import numpy as np
import ml_dtypes


def mxq(x, axis, fmt="e4m3"):
    dtype, down = {"e4m3": (ml_dtypes.float8_e4m3fn, 7), "e5m2": (ml_dtypes.float8_e5m2, 14)}[fmt]
    v = np.moveaxis(np.asarray(x, np.float32).astype(ml_dtypes.bfloat16).astype(np.float64), axis, -1)
    blocks = v.reshape(v.shape[:-1] + (-1, 32))
    amax = np.abs(blocks).max(-1, keepdims=True)
    byte = np.maximum(np.where(amax > 0, np.frexp(amax)[1] - 1 + 127, 0) - down, 1)
    scale = np.exp2(byte - 127.0)
    codes = (blocks / scale).astype(np.float32).astype(dtype).astype(np.float64)
    return np.moveaxis((codes * scale).reshape(v.shape), -1, axis)


WIDE = False


def mx_kscale(k):
    if not WIDE:
        return np.ones(k)
    levels = np.array([10, -10, 5, -5, 0])
    a = np.random.permutation(np.resize(levels, k // 512 * 4)).reshape(k // 512, 4)
    idx = np.arange(k)
    return np.exp2(a[idx // 512, idx % 128 // 32])


BF16 = ml_dtypes.bfloat16


def bf(x):
    return np.asarray(x, np.float32).astype(BF16)


def f64(x):
    return np.asarray(x).astype(np.float64)


E2M1 = np.array([0.0, 0.5, 1.0, 1.5, 2.0, 3.0, 4.0, 6.0, -0.0, -0.5, -1.0, -1.5, -2.0, -3.0, -4.0, -6.0])


def pack_weight(w, fmt):
    k, n = w.shape
    w = f64(bf(w)).reshape(k // 32, 32, n)
    amax = np.abs(w).max(1)
    if fmt == "e4m3":
        byte = np.frexp(amax)[1] - 1 + 127 - 7
    else:
        mant, ex = np.frexp(amax / 6.0)
        byte = np.where(mant > 0.5, ex, ex - 1) + 127
    byte = np.clip(np.where(amax > 0, byte, 1), 1, 254)
    scaled = (w * np.exp2(127.0 - byte)[:, None, :]).reshape(k, n).astype(np.float32)
    by_word = np.ascontiguousarray(scaled.reshape(k // 512, 128, 4, n).transpose(0, 1, 3, 2))
    if fmt == "e4m3":
        words = by_word.astype(ml_dtypes.float8_e4m3fn).view(np.uint8)
    else:
        c = by_word.astype(ml_dtypes.float4_e2m1fn).view(np.uint8) & 0xF
        words = c[..., 0::2] | (c[..., 1::2] << 4)
    return np.ascontiguousarray(words), np.ascontiguousarray(byte.astype(np.uint8).reshape(k // 512, 16, n))


def unpack_weight(words, scales, fmt):
    g, p, n, _ = words.shape
    if fmt == "e4m3":
        vals = np.ascontiguousarray(words).view(ml_dtypes.float8_e4m3fn).astype(np.float64)
    else:
        nib = np.empty((g, p, n, 4), np.uint8)
        nib[..., 0::2] = words & 0xF
        nib[..., 1::2] = words >> 4
        vals = E2M1[nib]
    vals = vals * np.repeat(np.exp2(scales.astype(np.float64) - 127.0), 8, axis=1)[..., None]
    return vals.transpose(0, 1, 3, 2).reshape(g * 512, n)

def pack4(w):
    words, scales = pack_weight(w, "e2m1")
    return words.reshape(words.shape[0], 128, -1), scales


def unpack4(words, scales):
    return unpack_weight(words.reshape(words.shape[0], 128, -1, 2), scales, "e2m1")


B, I, O, G = 4096, 512, 512, 2
K = I * G


def bspline_basis(d):
    inner = 1.0 - 6.0 * d * d + 6.0 * d * d * d
    outer = 2.0 * (1.0 - d) ** 3
    return np.where(d < 0.5, inner, np.where(d < 1.0, outer, np.zeros_like(d)))


def setup_inputs():
    g = np.linspace(-1.0, 1.0, G)
    s = mx_kscale(I)
    u = s / s.max()
    x_norm = bf(np.tanh(np.random.standard_normal((B, I))) * u)
    spline_weight = bf(np.random.standard_normal((O, I, G)) / np.sqrt(I))
    base_activation = np.random.standard_normal((O, I)) * 4.0 / np.sqrt(I) / u
    words, scales = pack4(base_activation.T)
    grid_points = bf(g + 0.1 * (g[1] - g[0]) * np.random.standard_normal(G))
    return {"x_norm": x_norm,
            "spline_weight": spline_weight,
            "base_activation_words": words,
            "base_activation_scales": scales,
            "grid_points": grid_points}


def reference(x_norm, spline_weight, base_activation_words, base_activation_scales, grid_points):
    t = f64(x_norm)
    d = np.abs(t[:, :, None] - f64(grid_points))
    basis = bspline_basis(d)
    spline_out = mxq(basis.reshape(B, K), 1, "e4m3") @ mxq(f64(spline_weight).reshape(O, K), 1, "e4m3").T
    base_out = mxq(t, 1, "e4m3") @ unpack4(base_activation_words, base_activation_scales)
    return spline_out + 0.1 * base_out

@@ -1,0 +1,257 @@
+from contextlib import ExitStack
+
+import concourse.mybir as mybir
+from concourse.masks import make_identity
+
+F32 = mybir.dt.float32
+BF16 = mybir.dt.bfloat16
+I32 = mybir.dt.int32
+U32 = mybir.dt.uint32
+U8 = mybir.dt.uint8
+FP8X4 = mybir.dt.float8_e4m3fn_x4
+FP4X4 = mybir.dt.float4_e2m1fn_x4
+ALU = mybir.AluOpType
+FUNC = mybir.ActivationFunctionType
+
+P = 128
+PACK = 4
+B, I, O, G = 4096, 512, 512, 2
+B_TILES = B // P
+J = 2
+CHUNKS = B_TILES // J
+W = J * P * PACK
+LOAD_TILES = 4
+O_TILES = O // P
+BASE_FACTOR = 0.1
+WEIGHT_COPIES = (8.0, 2.0)
+
+FLOPS = 2 * B * O * (I * G + I)
+
+
+def tile_advancedkanlayer_pa_t_kernel(
+    tc, x_norm, spline_weight, base_activation_words, base_activation_scales, grid_points, out
+):
+    nc = tc.nc
+    x_rows = x_norm.rearrange("(p n) i -> p n i", n=B_TILES)
+    out_rows = out.rearrange("(p n) o -> p n o", n=B_TILES)
+
+    with ExitStack() as ctx:
+        keep = ctx.enter_context(tc.tile_pool(name="keep", bufs=1))
+        work = ctx.enter_context(tc.tile_pool(name="work", bufs=2))
+        late = ctx.enter_context(tc.tile_pool(name="late", bufs=3))
+        turn_psum = ctx.enter_context(tc.psum_pool(name="turn_psum", bufs=2))
+        sum_psum = ctx.enter_context(tc.psum_pool(name="sum_psum", bufs=6))
+
+        grid_bf = keep.tile([P, G], BF16)
+        nc.sync.dma_start(out=grid_bf[:], in_=grid_points.partition_broadcast(P))
+        x_sb = keep.tile([P, B_TILES, I], BF16)
+        first = slice(0, LOAD_TILES)
+        nc.sync.dma_start(out=x_sb[:, first, :], in_=x_rows[:, first, :])
+        w_sb = keep.tile([P, O_TILES, I * G], BF16)
+        nc.sync.dma_start(
+            out=w_sb[:], in_=spline_weight.rearrange("(a p) i g -> p a (i g)", p=P)
+        )
+        w4_words = keep.tile([P, 2 * O], U8, align_bytes=64)
+        nc.sync.dma_start(
+            out=w4_words[:].bitcast(I32), in_=base_activation_words[0].bitcast(I32)
+        )
+        w4_scales = keep.tile([P, O], U8, align_bytes=64)
+        nc.vector.memset(w4_scales[:].bitcast(I32), 0)
+        for quad in range(4):
+            nc.sync.dma_start(
+                out=w4_scales[32 * quad : 32 * quad + 4, :].bitcast(I32),
+                in_=base_activation_scales[0, 4 * quad : 4 * quad + 4, :].bitcast(I32),
+            )
+        for n0 in range(LOAD_TILES, B_TILES, LOAD_TILES):
+            rows = slice(n0, n0 + LOAD_TILES)
+            nc.sync.dma_start(out=x_sb[:, rows, :], in_=x_rows[:, rows, :])
+
+        ident = keep.tile([P, P], F32)
+        make_identity(nc, ident[:])
+        neg_grid = keep.tile([P, G], F32)
+        nc.vector.tensor_scalar(
+            out=neg_grid[:], in0=grid_bf[:], scalar1=-1.0, scalar2=None, op0=ALU.mult
+        )
+        minus_one = keep.tile([P, 1], F32)
+        nc.vector.memset(minus_one[:], -1.0)
+
+        copies = len(WEIGHT_COPIES)
+        w_codes = keep.tile([P, copies, G * O], U32, align_bytes=64)
+        w_scales = keep.tile([P, copies, G * O], U8, align_bytes=64)
+
+        def prepare_spline_weight():
+            w_sorted = keep.tile([P, O_TILES, PACK, P], F32)
+            nc.vector.tensor_copy(
+                out=w_sorted[:],
+                in_=w_sb[:].bitcast(F32).rearrange("p a (q t) -> p a t q", t=PACK),
+            )
+            w_grouped = keep.tile([P, copies, G, O, PACK], BF16, align_bytes=64)
+            for a in range(O_TILES):
+                wt = turn_psum.tile([P, PACK, P], F32, tag="turned")
+                for t in range(PACK):
+                    nc.tensor.transpose(wt[:, t, :], w_sorted[:, a, t, :], ident[:])
+                nc.vector.tensor_scalar(
+                    out=w_grouped[:, 0, :, a * P : (a + 1) * P, :],
+                    in0=wt[:]
+                    .rearrange("q t o -> q (t o)")
+                    .bitcast(BF16)
+                    .rearrange("q (t o g) -> q g o t", t=PACK, g=G),
+                    scalar1=WEIGHT_COPIES[0],
+                    scalar2=None,
+                    op0=ALU.mult,
+                )
+            flat = w_grouped[:].rearrange("q s g o t -> q s (g o t)")
+            nc.vector.tensor_scalar(
+                out=flat[:, 1, :], in0=flat[:, 0, :],
+                scalar1=WEIGHT_COPIES[1] / WEIGHT_COPIES[0], scalar2=None, op0=ALU.mult,
+            )
+            for s in range(copies):
+                nc.vector.quantize_mx(
+                    out=w_codes[:, s, :].bitcast(FP8X4), scales=w_scales[:, s, :], in_=flat[:, s, :]
+                )
+
+        turned, grouped, dist, dist_sq, gap_sq = {}, {}, {}, {}, {}
+        x_codes, x_scales, basis_codes, basis_scales = {}, {}, {}, {}
+        basis, sums = {}, {}
+
+        def turn_x(c):
+            xt = turn_psum.tile([P, J, 2, P], F32, tag="turned")
+            for j in range(J):
+                words = x_sb[:, c * J + j, :].bitcast(F32)
+                for u in range(2):
+                    nc.tensor.transpose(xt[:, j, u, :], words[:, u : I // 2 : 2], ident[:])
+            turned[c] = xt
+
+        def regroup_x(c):
+            xg = late.tile([P, W], BF16, align_bytes=64, tag="xg")
+            nc.scalar.copy(
+                out=xg[:].bitcast(F32).rearrange("p (j b u) -> p j b u", j=J, u=2),
+                in_=turned[c][:].rearrange("p j u b -> p j b u"),
+            )
+            grouped[c] = xg
+
+        def distances(c):
+            d = work.tile([P, G, W], F32, tag="dist")
+            for g in range(G):
+                nc.scalar.activation(
+                    out=d[:, g, :], in_=grouped[c][:], func=FUNC.Abs,
+                    bias=neg_grid[:, g : g + 1], scale=1.0,
+                )
+            dist[c] = d
+
+        def squares(c):
+            s = work.tile([P, G * W], F32, tag="gap_sq")
+            nc.scalar.activation(
+                out=s[:], in_=dist[c][:].rearrange("p g w -> p (g w)"), func=FUNC.Square,
+                bias=minus_one[:], scale=1.0,
+            )
+            gap_sq[c] = s
+            q = work.tile([P, G, W], F32, tag="dist_sq")
+            for g in range(G):
+                nc.scalar.activation(
+                    out=q[:, g, :], in_=grouped[c][:], func=FUNC.Square,
+                    bias=neg_grid[:, g : g + 1], scale=1.0,
+                )
+            dist_sq[c] = q
+
+        def spline_basis(c):
+            d = dist[c][:].rearrange("p g w -> p (g w)")
+            neg_cube = work.tile([P, G * W], BF16, tag="neg_cube")
+            nc.vector.scalar_tensor_tensor(
+                out=neg_cube[:], in0=d, scalar=1.0, in1=gap_sq[c][:],
+                op0=ALU.subtract, op1=ALU.mult,
+            )
+            outer = work.tile([P, G * W], BF16, tag="outer")
+            nc.vector.tensor_scalar(
+                out=outer[:], in0=neg_cube[:], scalar1=-2.0, scalar2=0.0,
+                op0=ALU.mult, op1=ALU.max,
+            )
+            bend = work.tile([P, G * W], F32, tag="bend")
+            nc.vector.scalar_tensor_tensor(
+                out=bend[:], in0=d, scalar=1.0,
+                in1=dist_sq[c][:].rearrange("p g w -> p (g w)"),
+                op0=ALU.subtract, op1=ALU.mult,
+            )
+            inner = work.tile([P, G * W], BF16, tag="inner")
+            nc.vector.tensor_scalar(
+                out=inner[:], in0=bend[:], scalar1=6.0, scalar2=1.0, op0=ALU.mult, op1=ALU.add
+            )
+            n = work.tile([P, G * W], BF16, align_bytes=64, tag="basis")
+            nc.vector.tensor_tensor(out=n[:], in0=inner[:], in1=outer[:], op=ALU.min)
+            basis[c] = n
+
+        def quantise_x(c):
+            codes = late.tile([P, J * P], U32, align_bytes=64, tag="x_codes")
+            scales = late.tile([P, J * P], U8, align_bytes=64, tag="x_scales")
+            nc.vector.quantize_mx(
+                out=codes[:].bitcast(FP8X4), scales=scales[:], in_=grouped[c][:]
+            )
+            x_codes[c], x_scales[c] = codes, scales
+
+        def quantise_basis(c):
+            codes = late.tile([P, G * J * P], U32, align_bytes=64, tag="basis_codes")
+            scales = late.tile([P, G * J * P], U8, align_bytes=64, tag="basis_scales")
+            nc.vector.quantize_mx(out=codes[:].bitcast(FP8X4), scales=scales[:], in_=basis[c][:])
+            basis_codes[c], basis_scales[c] = codes, scales
+
+        def multiply(c):
+            for j in range(J):
+                acc = sum_psum.tile([P, O], F32, tag="acc")
+                rows = slice(j * P, (j + 1) * P)
+                nc.tensor.matmul_mx(
+                    out=acc[:],
+                    lhsT=x_codes[c][:, rows].bitcast(FP8X4),
+                    lhsT_scale=x_scales[c][:, rows],
+                    rhs=w4_words[:].bitcast(FP4X4),
+                    rhs_scale=w4_scales[:],
+                    start=True,
+                    stop=False,
+                )
+                for g in range(G):
+                    rows = slice((g * J + j) * P, (g * J + j + 1) * P)
+                    cols = slice(g * O, (g + 1) * O)
+                    for s in range(copies):
+                        nc.tensor.matmul_mx(
+                            out=acc[:],
+                            lhsT=basis_codes[c][:, rows].bitcast(FP8X4),
+                            lhsT_scale=basis_scales[c][:, rows],
+                            rhs=w_codes[:, s, cols].bitcast(FP8X4),
+                            rhs_scale=w_scales[:, s, cols],
+                            start=False,
+                            stop=(g == G - 1 and s == copies - 1),
+                        )
+                sums[c, j] = acc
+
+        def scale_and_store(c):
+            result = late.tile([P, J, O], F32, tag="result")
+            for j in range(J):
+                nc.scalar.mul(out=result[:, j, :], in_=sums[c, j][:], mul=BASE_FACTOR)
+            nc.sync.dma_start(out=out_rows[:, c * J : (c + 1) * J, :], in_=result[:])
+
+        def live(c):
+            return 0 <= c < CHUNKS
+
+        def step(c):
+            if live(c - 1):
+                multiply(c - 1)
+            if live(c + 2):
+                turn_x(c + 2)
+            if live(c + 1):
+                regroup_x(c + 1)
+                distances(c + 1)
+            if live(c - 1):
+                scale_and_store(c - 1)
+            if live(c + 1):
+                squares(c + 1)
+            if live(c):
+                spline_basis(c)
+            if live(c + 1):
+                quantise_x(c + 1)
+            if live(c):
+                quantise_basis(c)
+
+        step(-2)
+        step(-1)
+        prepare_spline_weight()
+        for c in range(CHUNKS + 1):
+            step(c)

@@ -1,3 +1,4 @@
+import math
 from contextlib import ExitStack
 
 import concourse.mybir as mybir
@@ -24,6 +25,8 @@ LOAD_TILES = 4
 O_TILES = O // P
 BASE_FACTOR = 0.1
 WEIGHT_COPIES = (8.0, 2.0)
+ROOT_6 = math.sqrt(6.0)
+ROOT_12 = math.sqrt(12.0)
 
 FLOPS = 2 * B * O * (I * G + I)
 
@@ -74,6 +77,14 @@ def tile_advancedkanlayer_pa_t_kernel(
         )
         minus_one = keep.tile([P, 1], F32)
         nc.vector.memset(minus_one[:], -1.0)
+        cube_bias = keep.tile([P, 1], F32)
+        nc.vector.tensor_scalar(
+            out=cube_bias[:], in0=minus_one[:], scalar1=ROOT_6, scalar2=None, op0=ALU.mult
+        )
+        bowl_bias = keep.tile([P, 1], F32)
+        nc.vector.tensor_scalar(
+            out=bowl_bias[:], in0=minus_one[:], scalar1=0.75 * ROOT_12, scalar2=None, op0=ALU.mult
+        )
 
         copies = len(WEIGHT_COPIES)
         w_codes = keep.tile([P, copies, G * O], U32, align_bytes=64)
@@ -110,7 +121,7 @@ def tile_advancedkanlayer_pa_t_kernel(
                     out=w_codes[:, s, :].bitcast(FP8X4), scales=w_scales[:, s, :], in_=flat[:, s, :]
                 )
 
-        turned, grouped, dist, dist_sq, gap_sq = {}, {}, {}, {}, {}
+        turned, grouped, dist, bowl, gap_sq = {}, {}, {}, {}, {}
         x_codes, x_scales, basis_codes, basis_scales = {}, {}, {}, {}
         basis, sums = {}, {}
 
@@ -140,41 +151,28 @@ def tile_advancedkanlayer_pa_t_kernel(
             dist[c] = d
 
         def squares(c):
+            d = dist[c][:].rearrange("p g w -> p (g w)")
             s = work.tile([P, G * W], F32, tag="gap_sq")
-            nc.scalar.activation(
-                out=s[:], in_=dist[c][:].rearrange("p g w -> p (g w)"), func=FUNC.Square,
-                bias=minus_one[:], scale=1.0,
-            )
+            nc.scalar.activation(out=s[:], in_=d, func=FUNC.Square, bias=cube_bias[:], scale=ROOT_6)
             gap_sq[c] = s
-            q = work.tile([P, G, W], F32, tag="dist_sq")
-            for g in range(G):
-                nc.scalar.activation(
-                    out=q[:, g, :], in_=grouped[c][:], func=FUNC.Square,
-                    bias=neg_grid[:, g : g + 1], scale=1.0,
-                )
-            dist_sq[c] = q
+            q = work.tile([P, G * W], F32, tag="bowl")
+            nc.scalar.activation(out=q[:], in_=d, func=FUNC.Square, bias=bowl_bias[:], scale=ROOT_12)
+            bowl[c] = q
 
         def spline_basis(c):
-            d = dist[c][:].rearrange("p g w -> p (g w)")
-            neg_cube = work.tile([P, G * W], BF16, tag="neg_cube")
+            cube = work.tile([P, G * W], F32, tag="cube")
             nc.vector.scalar_tensor_tensor(
-                out=neg_cube[:], in0=d, scalar=1.0, in1=gap_sq[c][:],
-                op0=ALU.subtract, op1=ALU.mult,
+                out=cube[:], in0=dist[c][:].rearrange("p g w -> p (g w)"), scalar=1.0,
+                in1=gap_sq[c][:], op0=ALU.subtract, op1=ALU.mult,
+            )
+            inner = work.tile([P, G * W], BF16, tag="inner")
+            nc.vector.scalar_tensor_tensor(
+                out=inner[:], in0=bowl[c][:], scalar=0.25, in1=cube[:], op0=ALU.add, op1=ALU.add
             )
             outer = work.tile([P, G * W], BF16, tag="outer")
             nc.vector.tensor_scalar(
-                out=outer[:], in0=neg_cube[:], scalar1=-2.0, scalar2=0.0,
+                out=outer[:], in0=cube[:], scalar1=-1.0 / 3.0, scalar2=0.0,
                 op0=ALU.mult, op1=ALU.max,
-            )
-            bend = work.tile([P, G * W], F32, tag="bend")
-            nc.vector.scalar_tensor_tensor(
-                out=bend[:], in0=d, scalar=1.0,
-                in1=dist_sq[c][:].rearrange("p g w -> p (g w)"),
-                op0=ALU.subtract, op1=ALU.mult,
-            )
-            inner = work.tile([P, G * W], BF16, tag="inner")
-            nc.vector.tensor_scalar(
-                out=inner[:], in0=bend[:], scalar1=6.0, scalar2=1.0, op0=ALU.mult, op1=ALU.add
             )
             n = work.tile([P, G * W], BF16, align_bytes=64, tag="basis")
             nc.vector.tensor_tensor(out=n[:], in0=inner[:], in1=outer[:], op=ALU.min)

@@ -27,6 +27,7 @@ BASE_FACTOR = 0.1
 WEIGHT_COPIES = (8.0, 2.0)
 ROOT_6 = math.sqrt(6.0)
 ROOT_12 = math.sqrt(12.0)
+VECTOR_SHARE = 4
 
 FLOPS = 2 * B * O * (I * G + I)
 
@@ -37,6 +38,7 @@ def tile_advancedkanlayer_pa_t_kernel(
     nc = tc.nc
     x_rows = x_norm.rearrange("(p n) i -> p n i", n=B_TILES)
     out_rows = out.rearrange("(p n) o -> p n o", n=B_TILES)
+    copies = len(WEIGHT_COPIES)
 
     with ExitStack() as ctx:
         keep = ctx.enter_context(tc.tile_pool(name="keep", bufs=1))
@@ -44,16 +46,17 @@ def tile_advancedkanlayer_pa_t_kernel(
         late = ctx.enter_context(tc.tile_pool(name="late", bufs=3))
         turn_psum = ctx.enter_context(tc.psum_pool(name="turn_psum", bufs=2))
         sum_psum = ctx.enter_context(tc.psum_pool(name="sum_psum", bufs=6))
+        ctx.enter_context(tc.manual_schedule())
 
         grid_bf = keep.tile([P, G], BF16)
         nc.sync.dma_start(out=grid_bf[:], in_=grid_points.partition_broadcast(P))
         x_sb = keep.tile([P, B_TILES, I], BF16)
-        first = slice(0, LOAD_TILES)
-        nc.sync.dma_start(out=x_sb[:, first, :], in_=x_rows[:, first, :])
+        nc.sync.dma_start(out=x_sb[:, 0:J, :], in_=x_rows[:, 0:J, :])
         w_sb = keep.tile([P, O_TILES, I * G], BF16)
-        nc.sync.dma_start(
-            out=w_sb[:], in_=spline_weight.rearrange("(a p) i g -> p a (i g)", p=P)
-        )
+        w_rows = spline_weight.rearrange("(a p) i g -> p a (i g)", p=P)
+        for a in range(O_TILES):
+            nc.sync.dma_start(out=w_sb[:, a, :], in_=w_rows[:, a, :])
+        nc.sync.dma_start(out=x_sb[:, J:LOAD_TILES, :], in_=x_rows[:, J:LOAD_TILES, :])
         w4_words = keep.tile([P, 2 * O], U8, align_bytes=64)
         nc.sync.dma_start(
             out=w4_words[:].bitcast(I32), in_=base_activation_words[0].bitcast(I32)
@@ -71,10 +74,6 @@ def tile_advancedkanlayer_pa_t_kernel(
 
         ident = keep.tile([P, P], F32)
         make_identity(nc, ident[:])
-        neg_grid = keep.tile([P, G], F32)
-        nc.vector.tensor_scalar(
-            out=neg_grid[:], in0=grid_bf[:], scalar1=-1.0, scalar2=None, op0=ALU.mult
-        )
         minus_one = keep.tile([P, 1], F32)
         nc.vector.memset(minus_one[:], -1.0)
         cube_bias = keep.tile([P, 1], F32)
@@ -85,17 +84,21 @@ def tile_advancedkanlayer_pa_t_kernel(
         nc.vector.tensor_scalar(
             out=bowl_bias[:], in0=minus_one[:], scalar1=0.75 * ROOT_12, scalar2=None, op0=ALU.mult
         )
+        neg_grid = keep.tile([P, G], F32)
+        nc.vector.tensor_scalar(
+            out=neg_grid[:], in0=grid_bf[:], scalar1=-1.0, scalar2=None, op0=ALU.mult
+        )
 
-        copies = len(WEIGHT_COPIES)
         w_codes = keep.tile([P, copies, G * O], U32, align_bytes=64)
         w_scales = keep.tile([P, copies, G * O], U8, align_bytes=64)
 
         def prepare_spline_weight():
             w_sorted = keep.tile([P, O_TILES, PACK, P], F32)
-            nc.vector.tensor_copy(
-                out=w_sorted[:],
-                in_=w_sb[:].bitcast(F32).rearrange("p a (q t) -> p a t q", t=PACK),
-            )
+            for a in range(O_TILES):
+                nc.vector.tensor_copy(
+                    out=w_sorted[:, a, :, :],
+                    in_=w_sb[:, a, :].bitcast(F32).rearrange("p (q t) -> p t q", t=PACK),
+                )
             w_grouped = keep.tile([P, copies, G, O, PACK], BF16, align_bytes=64)
             for a in range(O_TILES):
                 wt = turn_psum.tile([P, PACK, P], F32, tag="turned")
@@ -123,7 +126,7 @@ def tile_advancedkanlayer_pa_t_kernel(
 
         turned, grouped, dist, bowl, gap_sq = {}, {}, {}, {}, {}
         x_codes, x_scales, basis_codes, basis_scales = {}, {}, {}, {}
-        basis, sums = {}, {}
+        cube, inner, outer, basis, sums, result = {}, {}, {}, {}, {}, {}
 
         def turn_x(c):
             xt = turn_psum.tile([P, J, 2, P], F32, tag="turned")
@@ -150,37 +153,55 @@ def tile_advancedkanlayer_pa_t_kernel(
                 )
             dist[c] = d
 
-        def squares(c):
-            d = dist[c][:].rearrange("p g w -> p (g w)")
+
+        def gap_square(c):
             s = work.tile([P, G * W], F32, tag="gap_sq")
-            nc.scalar.activation(out=s[:], in_=d, func=FUNC.Square, bias=cube_bias[:], scale=ROOT_6)
+            nc.scalar.activation(
+                out=s[:], in_=dist[c][:].rearrange("p g w -> p (g w)"), func=FUNC.Square,
+                bias=cube_bias[:], scale=ROOT_6,
+            )
             gap_sq[c] = s
+
+        def bowl_square(c):
             q = work.tile([P, G * W], F32, tag="bowl")
-            nc.scalar.activation(out=q[:], in_=d, func=FUNC.Square, bias=bowl_bias[:], scale=ROOT_12)
+            nc.scalar.activation(
+                out=q[:], in_=dist[c][:].rearrange("p g w -> p (g w)"), func=FUNC.Square,
+                bias=bowl_bias[:], scale=ROOT_12,
+            )
             bowl[c] = q
 
-        def spline_basis(c):
-            cube = work.tile([P, G * W], F32, tag="cube")
+        def cube_of_gap(c):
+            m3 = work.tile([P, G * W], F32, tag="cube")
             nc.vector.scalar_tensor_tensor(
-                out=cube[:], in0=dist[c][:].rearrange("p g w -> p (g w)"), scalar=1.0,
+                out=m3[:], in0=dist[c][:].rearrange("p g w -> p (g w)"), scalar=1.0,
                 in1=gap_sq[c][:], op0=ALU.subtract, op1=ALU.mult,
             )
-            inner = work.tile([P, G * W], BF16, tag="inner")
+            cube[c] = m3
+
+        def inner_piece(c):
+            piece = work.tile([P, G * W], BF16, tag="inner")
             nc.vector.scalar_tensor_tensor(
-                out=inner[:], in0=bowl[c][:], scalar=0.25, in1=cube[:], op0=ALU.add, op1=ALU.add
+                out=piece[:], in0=bowl[c][:], scalar=0.25, in1=cube[c][:],
+                op0=ALU.add, op1=ALU.add,
             )
-            outer = work.tile([P, G * W], BF16, tag="outer")
+            inner[c] = piece
+
+        def outer_piece(c):
+            piece = work.tile([P, G * W], BF16, tag="outer")
             nc.vector.tensor_scalar(
-                out=outer[:], in0=cube[:], scalar1=-1.0 / 3.0, scalar2=0.0,
+                out=piece[:], in0=cube[c][:], scalar1=-1.0 / 3.0, scalar2=0.0,
                 op0=ALU.mult, op1=ALU.max,
             )
+            outer[c] = piece
+
+        def minimum(c):
             n = work.tile([P, G * W], BF16, align_bytes=64, tag="basis")
-            nc.vector.tensor_tensor(out=n[:], in0=inner[:], in1=outer[:], op=ALU.min)
+            nc.vector.tensor_tensor(out=n[:], in0=inner[c][:], in1=outer[c][:], op=ALU.min)
             basis[c] = n
 
         def quantise_x(c):
-            codes = late.tile([P, J * P], U32, align_bytes=64, tag="x_codes")
-            scales = late.tile([P, J * P], U8, align_bytes=64, tag="x_scales")
+            codes = late.tile([P, J * P], U32, align_bytes=64, tag="x_codes", bufs=4)
+            scales = late.tile([P, J * P], U8, align_bytes=64, tag="x_scales", bufs=4)
             nc.vector.quantize_mx(
                 out=codes[:].bitcast(FP8X4), scales=scales[:], in_=grouped[c][:]
             )
@@ -220,36 +241,48 @@ def tile_advancedkanlayer_pa_t_kernel(
                         )
                 sums[c, j] = acc
 
-        def scale_and_store(c):
-            result = late.tile([P, J, O], F32, tag="result")
-            for j in range(J):
-                nc.scalar.mul(out=result[:, j, :], in_=sums[c, j][:], mul=BASE_FACTOR)
-            nc.sync.dma_start(out=out_rows[:, c * J : (c + 1) * J, :], in_=result[:])
+        def leave_psum(c, j):
+            if (c * J + j) % VECTOR_SHARE == VECTOR_SHARE - 1:
+                nc.vector.tensor_scalar(
+                    out=result[c][:, j, :], in0=sums[c, j][:], scalar1=BASE_FACTOR, scalar2=None,
+                    op0=ALU.mult,
+                )
+            else:
+                nc.scalar.mul(out=result[c][:, j, :], in_=sums[c, j][:], mul=BASE_FACTOR)
 
-        def live(c):
-            return 0 <= c < CHUNKS
+        def leave_first(c):
+            scaled = late.tile([P, J, O], F32, tag="result")
+            result[c] = scaled
+            leave_psum(c, 0)
+
+        def leave_second(c):
+            leave_psum(c, 1)
+
+        def store(c):
+            nc.sync.dma_start(out=out_rows[:, c * J : (c + 1) * J, :], in_=result[c][:])
+
+        def run(stage, c):
+            if 0 <= c < CHUNKS:
+                stage(c)
 
         def step(c):
-            if live(c - 1):
-                multiply(c - 1)
-            if live(c + 2):
-                turn_x(c + 2)
-            if live(c + 1):
-                regroup_x(c + 1)
-                distances(c + 1)
-            if live(c - 1):
-                scale_and_store(c - 1)
-            if live(c + 1):
-                squares(c + 1)
-            if live(c):
-                spline_basis(c)
-            if live(c + 1):
-                quantise_x(c + 1)
-            if live(c):
-                quantise_basis(c)
+            run(turn_x, c + 2)
+            run(multiply, c - 2)
+            run(distances, c + 1)
+            run(cube_of_gap, c)
+            run(leave_first, c - 3)
+            run(minimum, c - 1)
+            run(gap_square, c + 1)
+            run(inner_piece, c)
+            run(leave_second, c - 3)
+            run(quantise_x, c + 1)
+            run(bowl_square, c + 1)
+            run(outer_piece, c)
+            run(store, c - 3)
+            run(regroup_x, c + 2)
+            run(quantise_basis, c - 1)
 
         step(-2)
-        step(-1)
         prepare_spline_weight()
-        for c in range(CHUNKS + 1):
+        for c in range(-1, CHUNKS + 3):
             step(c)

@@ -18,9 +18,10 @@ P = 128
 PACK = 4
 B, I, O, G = 4096, 512, 512, 2
 B_TILES = B // P
-J = 2
-CHUNKS = B_TILES // J
-W = J * P * PACK
+CHUNK_TILES = (2,) * 15 + (1, 1)
+CHUNKS = len(CHUNK_TILES)
+FIRST_TILE = tuple(sum(CHUNK_TILES[:c]) for c in range(CHUNKS))
+TILE_W = P * PACK
 LOAD_TILES = 4
 O_TILES = O // P
 BASE_FACTOR = 0.1
@@ -28,6 +29,7 @@ WEIGHT_COPIES = (8.0, 2.0)
 ROOT_6 = math.sqrt(6.0)
 ROOT_12 = math.sqrt(12.0)
 VECTOR_SHARE = 4
+SCALAR_ONLY_FROM = B_TILES - 6
 
 FLOPS = 2 * B * O * (I * G + I)
 
@@ -51,12 +53,13 @@ def tile_advancedkanlayer_pa_t_kernel(
         grid_bf = keep.tile([P, G], BF16)
         nc.sync.dma_start(out=grid_bf[:], in_=grid_points.partition_broadcast(P))
         x_sb = keep.tile([P, B_TILES, I], BF16)
-        nc.sync.dma_start(out=x_sb[:, 0:J, :], in_=x_rows[:, 0:J, :])
+        head = CHUNK_TILES[0]
+        nc.sync.dma_start(out=x_sb[:, 0:head, :], in_=x_rows[:, 0:head, :])
         w_sb = keep.tile([P, O_TILES, I * G], BF16)
         w_rows = spline_weight.rearrange("(a p) i g -> p a (i g)", p=P)
         for a in range(O_TILES):
             nc.sync.dma_start(out=w_sb[:, a, :], in_=w_rows[:, a, :])
-        nc.sync.dma_start(out=x_sb[:, J:LOAD_TILES, :], in_=x_rows[:, J:LOAD_TILES, :])
+        nc.sync.dma_start(out=x_sb[:, head:LOAD_TILES, :], in_=x_rows[:, head:LOAD_TILES, :])
         w4_words = keep.tile([P, 2 * O], U8, align_bytes=64)
         nc.sync.dma_start(
             out=w4_words[:].bitcast(I32), in_=base_activation_words[0].bitcast(I32)
@@ -93,17 +96,12 @@ def tile_advancedkanlayer_pa_t_kernel(
         w_scales = keep.tile([P, copies, G * O], U8, align_bytes=64)
 
         def prepare_spline_weight():
-            w_sorted = keep.tile([P, O_TILES, PACK, P], F32)
-            for a in range(O_TILES):
-                nc.vector.tensor_copy(
-                    out=w_sorted[:, a, :, :],
-                    in_=w_sb[:, a, :].bitcast(F32).rearrange("p (q t) -> p t q", t=PACK),
-                )
             w_grouped = keep.tile([P, copies, G, O, PACK], BF16, align_bytes=64)
             for a in range(O_TILES):
                 wt = turn_psum.tile([P, PACK, P], F32, tag="turned")
+                w_words = w_sb[:, a, :].bitcast(F32)
                 for t in range(PACK):
-                    nc.tensor.transpose(wt[:, t, :], w_sorted[:, a, t, :], ident[:])
+                    nc.tensor.transpose(wt[:, t, :], w_words[:, t : I : PACK], ident[:])
                 nc.vector.tensor_scalar(
                     out=w_grouped[:, 0, :, a * P : (a + 1) * P, :],
                     in0=wt[:]
@@ -129,23 +127,23 @@ def tile_advancedkanlayer_pa_t_kernel(
         cube, inner, outer, basis, sums, result = {}, {}, {}, {}, {}, {}
 
         def turn_x(c):
-            xt = turn_psum.tile([P, J, 2, P], F32, tag="turned")
-            for j in range(J):
-                words = x_sb[:, c * J + j, :].bitcast(F32)
+            xt = turn_psum.tile([P, CHUNK_TILES[c], 2, P], F32, tag="turned")
+            for j in range(CHUNK_TILES[c]):
+                words = x_sb[:, FIRST_TILE[c] + j, :].bitcast(F32)
                 for u in range(2):
                     nc.tensor.transpose(xt[:, j, u, :], words[:, u : I // 2 : 2], ident[:])
             turned[c] = xt
 
         def regroup_x(c):
-            xg = late.tile([P, W], BF16, align_bytes=64, tag="xg")
+            xg = late.tile([P, CHUNK_TILES[c] * TILE_W], BF16, align_bytes=64, tag="xg")
             nc.scalar.copy(
-                out=xg[:].bitcast(F32).rearrange("p (j b u) -> p j b u", j=J, u=2),
+                out=xg[:].bitcast(F32).rearrange("p (j b u) -> p j b u", j=CHUNK_TILES[c], u=2),
                 in_=turned[c][:].rearrange("p j u b -> p j b u"),
             )
             grouped[c] = xg
 
         def distances(c):
-            d = work.tile([P, G, W], F32, tag="dist")
+            d = work.tile([P, G, CHUNK_TILES[c] * TILE_W], F32, tag="dist")
             for g in range(G):
                 nc.scalar.activation(
                     out=d[:, g, :], in_=grouped[c][:], func=FUNC.Abs,
@@ -155,7 +153,7 @@ def tile_advancedkanlayer_pa_t_kernel(
 
 
         def gap_square(c):
-            s = work.tile([P, G * W], F32, tag="gap_sq")
+            s = work.tile([P, G * CHUNK_TILES[c] * TILE_W], F32, tag="gap_sq")
             nc.scalar.activation(
                 out=s[:], in_=dist[c][:].rearrange("p g w -> p (g w)"), func=FUNC.Square,
                 bias=cube_bias[:], scale=ROOT_6,
@@ -163,7 +161,7 @@ def tile_advancedkanlayer_pa_t_kernel(
             gap_sq[c] = s
 
         def bowl_square(c):
-            q = work.tile([P, G * W], F32, tag="bowl")
+            q = work.tile([P, G * CHUNK_TILES[c] * TILE_W], F32, tag="bowl")
             nc.scalar.activation(
                 out=q[:], in_=dist[c][:].rearrange("p g w -> p (g w)"), func=FUNC.Square,
                 bias=bowl_bias[:], scale=ROOT_12,
@@ -171,7 +169,7 @@ def tile_advancedkanlayer_pa_t_kernel(
             bowl[c] = q
 
         def cube_of_gap(c):
-            m3 = work.tile([P, G * W], F32, tag="cube")
+            m3 = work.tile([P, G * CHUNK_TILES[c] * TILE_W], F32, tag="cube")
             nc.vector.scalar_tensor_tensor(
                 out=m3[:], in0=dist[c][:].rearrange("p g w -> p (g w)"), scalar=1.0,
                 in1=gap_sq[c][:], op0=ALU.subtract, op1=ALU.mult,
@@ -179,7 +177,7 @@ def tile_advancedkanlayer_pa_t_kernel(
             cube[c] = m3
 
         def inner_piece(c):
-            piece = work.tile([P, G * W], BF16, tag="inner")
+            piece = work.tile([P, G * CHUNK_TILES[c] * TILE_W], BF16, tag="inner")
             nc.vector.scalar_tensor_tensor(
                 out=piece[:], in0=bowl[c][:], scalar=0.25, in1=cube[c][:],
                 op0=ALU.add, op1=ALU.add,
@@ -187,7 +185,7 @@ def tile_advancedkanlayer_pa_t_kernel(
             inner[c] = piece
 
         def outer_piece(c):
-            piece = work.tile([P, G * W], BF16, tag="outer")
+            piece = work.tile([P, G * CHUNK_TILES[c] * TILE_W], BF16, tag="outer")
             nc.vector.tensor_scalar(
                 out=piece[:], in0=cube[c][:], scalar1=-1.0 / 3.0, scalar2=0.0,
                 op0=ALU.mult, op1=ALU.max,
@@ -195,26 +193,27 @@ def tile_advancedkanlayer_pa_t_kernel(
             outer[c] = piece
 
         def minimum(c):
-            n = work.tile([P, G * W], BF16, align_bytes=64, tag="basis")
+            n = work.tile([P, G * CHUNK_TILES[c] * TILE_W], BF16, align_bytes=64, tag="basis")
             nc.vector.tensor_tensor(out=n[:], in0=inner[c][:], in1=outer[c][:], op=ALU.min)
             basis[c] = n
 
         def quantise_x(c):
-            codes = late.tile([P, J * P], U32, align_bytes=64, tag="x_codes", bufs=4)
-            scales = late.tile([P, J * P], U8, align_bytes=64, tag="x_scales", bufs=4)
+            codes = late.tile([P, CHUNK_TILES[c] * P], U32, align_bytes=64, tag="x_codes", bufs=4)
+            scales = late.tile([P, CHUNK_TILES[c] * P], U8, align_bytes=64, tag="x_scales", bufs=4)
             nc.vector.quantize_mx(
                 out=codes[:].bitcast(FP8X4), scales=scales[:], in_=grouped[c][:]
             )
             x_codes[c], x_scales[c] = codes, scales
 
         def quantise_basis(c):
-            codes = late.tile([P, G * J * P], U32, align_bytes=64, tag="basis_codes")
-            scales = late.tile([P, G * J * P], U8, align_bytes=64, tag="basis_scales")
+            codes = late.tile([P, G * CHUNK_TILES[c] * P], U32, align_bytes=64, tag="basis_codes")
+            scales = late.tile([P, G * CHUNK_TILES[c] * P], U8, align_bytes=64, tag="basis_scales")
             nc.vector.quantize_mx(out=codes[:].bitcast(FP8X4), scales=scales[:], in_=basis[c][:])
             basis_codes[c], basis_scales[c] = codes, scales
 
         def multiply(c):
-            for j in range(J):
+            tiles = CHUNK_TILES[c]
+            for j in range(tiles):
                 acc = sum_psum.tile([P, O], F32, tag="acc")
                 rows = slice(j * P, (j + 1) * P)
                 nc.tensor.matmul_mx(
@@ -227,7 +226,7 @@ def tile_advancedkanlayer_pa_t_kernel(
                     stop=False,
                 )
                 for g in range(G):
-                    rows = slice((g * J + j) * P, (g * J + j + 1) * P)
+                    rows = slice((g * tiles + j) * P, (g * tiles + j + 1) * P)
                     cols = slice(g * O, (g + 1) * O)
                     for s in range(copies):
                         nc.tensor.matmul_mx(
@@ -242,7 +241,8 @@ def tile_advancedkanlayer_pa_t_kernel(
                 sums[c, j] = acc
 
         def leave_psum(c, j):
-            if (c * J + j) % VECTOR_SHARE == VECTOR_SHARE - 1:
+            n = FIRST_TILE[c] + j
+            if n % VECTOR_SHARE == VECTOR_SHARE - 1 and n < SCALAR_ONLY_FROM:
                 nc.vector.tensor_scalar(
                     out=result[c][:, j, :], in0=sums[c, j][:], scalar1=BASE_FACTOR, scalar2=None,
                     op0=ALU.mult,
@@ -251,15 +251,17 @@ def tile_advancedkanlayer_pa_t_kernel(
                 nc.scalar.mul(out=result[c][:, j, :], in_=sums[c, j][:], mul=BASE_FACTOR)
 
         def leave_first(c):
-            scaled = late.tile([P, J, O], F32, tag="result")
+            scaled = late.tile([P, CHUNK_TILES[c], O], F32, tag="result")
             result[c] = scaled
             leave_psum(c, 0)
 
         def leave_second(c):
-            leave_psum(c, 1)
+            if CHUNK_TILES[c] > 1:
+                leave_psum(c, 1)
 
         def store(c):
-            nc.sync.dma_start(out=out_rows[:, c * J : (c + 1) * J, :], in_=result[c][:])
+            rows = slice(FIRST_TILE[c], FIRST_TILE[c] + CHUNK_TILES[c])
+            nc.sync.dma_start(out=out_rows[:, rows, :], in_=result[c][:])
 
         def run(stage, c):
             if 0 <= c < CHUNKS:

@@ -30,6 +30,7 @@ ROOT_6 = math.sqrt(6.0)
 ROOT_12 = math.sqrt(12.0)
 VECTOR_SHARE = 4
 SCALAR_ONLY_FROM = B_TILES - 6
+SCALAR_OUTER_CHUNKS = 2
 
 FLOPS = 2 * B * O * (I * G + I)
 
@@ -186,10 +187,13 @@ def tile_advancedkanlayer_pa_t_kernel(
 
         def outer_piece(c):
             piece = work.tile([P, G * CHUNK_TILES[c] * TILE_W], BF16, tag="outer")
-            nc.vector.tensor_scalar(
-                out=piece[:], in0=cube[c][:], scalar1=-1.0 / 3.0, scalar2=0.0,
-                op0=ALU.mult, op1=ALU.max,
-            )
+            if c >= CHUNKS - SCALAR_OUTER_CHUNKS:
+                nc.scalar.activation(out=piece[:], in_=cube[c][:], func=FUNC.Relu, scale=-1.0 / 3.0)
+            else:
+                nc.vector.tensor_scalar(
+                    out=piece[:], in0=cube[c][:], scalar1=-1.0 / 3.0, scalar2=0.0,
+                    op0=ALU.mult, op1=ALU.max,
+                )
             outer[c] = piece
 
         def minimum(c):
@@ -272,16 +276,16 @@ def tile_advancedkanlayer_pa_t_kernel(
             run(multiply, c - 2)
             run(distances, c + 1)
             run(cube_of_gap, c)
-            run(leave_first, c - 3)
+            run(regroup_x, c + 2)
             run(minimum, c - 1)
             run(gap_square, c + 1)
             run(inner_piece, c)
-            run(leave_second, c - 3)
+            run(leave_first, c - 3)
             run(quantise_x, c + 1)
             run(bowl_square, c + 1)
             run(outer_piece, c)
+            run(leave_second, c - 3)
             run(store, c - 3)
-            run(regroup_x, c + 2)
             run(quantise_basis, c - 1)
 
         step(-2)

@@ -252,7 +252,9 @@ def tile_advancedkanlayer_pa_t_kernel(
                     op0=ALU.mult,
                 )
             else:
-                nc.scalar.mul(out=result[c][:, j, :], in_=sums[c, j][:], mul=BASE_FACTOR)
+                nc.scalar.activation(
+                    out=result[c][:, j, :], in_=sums[c, j][:], func=FUNC.Copy, scale=BASE_FACTOR
+                )
 
         def leave_first(c):
             scaled = late.tile([P, CHUNK_TILES[c], O], F32, tag="result")

import math
from contextlib import ExitStack

import concourse.mybir as mybir
from concourse.masks import make_identity

F32 = mybir.dt.float32
BF16 = mybir.dt.bfloat16
I32 = mybir.dt.int32
U32 = mybir.dt.uint32
U8 = mybir.dt.uint8
FP8X4 = mybir.dt.float8_e4m3fn_x4
FP4X4 = mybir.dt.float4_e2m1fn_x4
ALU = mybir.AluOpType
FUNC = mybir.ActivationFunctionType

P = 128
PACK = 4
B, I, O, G = 4096, 512, 512, 2
B_TILES = B // P
CHUNK_TILES = (2,) * 15 + (1, 1)
CHUNKS = len(CHUNK_TILES)
FIRST_TILE = tuple(sum(CHUNK_TILES[:c]) for c in range(CHUNKS))
TILE_W = P * PACK
LOAD_TILES = 4
O_TILES = O // P
BASE_FACTOR = 0.1
WEIGHT_COPIES = (8.0, 2.0)
ROOT_6 = math.sqrt(6.0)
ROOT_12 = math.sqrt(12.0)
VECTOR_SHARE = 4
SCALAR_ONLY_FROM = B_TILES - 6
SCALAR_OUTER_CHUNKS = 2

FLOPS = 2 * B * O * (I * G + I)


def tile_advancedkanlayer_pa_t_kernel(
    tc, x_norm, spline_weight, base_activation_words, base_activation_scales, grid_points, out
):
    nc = tc.nc
    x_rows = x_norm.rearrange("(p n) i -> p n i", n=B_TILES)
    out_rows = out.rearrange("(p n) o -> p n o", n=B_TILES)
    copies = len(WEIGHT_COPIES)

    with ExitStack() as ctx:
        keep = ctx.enter_context(tc.tile_pool(name="keep", bufs=1))
        work = ctx.enter_context(tc.tile_pool(name="work", bufs=2))
        late = ctx.enter_context(tc.tile_pool(name="late", bufs=3))
        turn_psum = ctx.enter_context(tc.psum_pool(name="turn_psum", bufs=2))
        sum_psum = ctx.enter_context(tc.psum_pool(name="sum_psum", bufs=6))
        ctx.enter_context(tc.manual_schedule())

        grid_bf = keep.tile([P, G], BF16)
        nc.sync.dma_start(out=grid_bf[:], in_=grid_points.partition_broadcast(P))
        x_sb = keep.tile([P, B_TILES, I], BF16)
        head = CHUNK_TILES[0]
        nc.sync.dma_start(out=x_sb[:, 0:head, :], in_=x_rows[:, 0:head, :])
        w_sb = keep.tile([P, O_TILES, I * G], BF16)
        w_rows = spline_weight.rearrange("(a p) i g -> p a (i g)", p=P)
        for a in range(O_TILES):
            nc.sync.dma_start(out=w_sb[:, a, :], in_=w_rows[:, a, :])
        nc.sync.dma_start(out=x_sb[:, head:LOAD_TILES, :], in_=x_rows[:, head:LOAD_TILES, :])
        w4_words = keep.tile([P, 2 * O], U8, align_bytes=64)
        nc.sync.dma_start(
            out=w4_words[:].bitcast(I32), in_=base_activation_words[0].bitcast(I32)
        )
        w4_scales = keep.tile([P, O], U8, align_bytes=64)
        nc.vector.memset(w4_scales[:].bitcast(I32), 0)
        for quad in range(4):
            nc.sync.dma_start(
                out=w4_scales[32 * quad : 32 * quad + 4, :].bitcast(I32),
                in_=base_activation_scales[0, 4 * quad : 4 * quad + 4, :].bitcast(I32),
            )
        for n0 in range(LOAD_TILES, B_TILES, LOAD_TILES):
            rows = slice(n0, n0 + LOAD_TILES)
            nc.sync.dma_start(out=x_sb[:, rows, :], in_=x_rows[:, rows, :])

        ident = keep.tile([P, P], F32)
        make_identity(nc, ident[:])
        minus_one = keep.tile([P, 1], F32)
        nc.vector.memset(minus_one[:], -1.0)
        cube_bias = keep.tile([P, 1], F32)
        nc.vector.tensor_scalar(
            out=cube_bias[:], in0=minus_one[:], scalar1=ROOT_6, scalar2=None, op0=ALU.mult
        )
        bowl_bias = keep.tile([P, 1], F32)
        nc.vector.tensor_scalar(
            out=bowl_bias[:], in0=minus_one[:], scalar1=0.75 * ROOT_12, scalar2=None, op0=ALU.mult
        )
        neg_grid = keep.tile([P, G], F32)
        nc.vector.tensor_scalar(
            out=neg_grid[:], in0=grid_bf[:], scalar1=-1.0, scalar2=None, op0=ALU.mult
        )

        w_codes = keep.tile([P, copies, G * O], U32, align_bytes=64)
        w_scales = keep.tile([P, copies, G * O], U8, align_bytes=64)

        def prepare_spline_weight():
            w_grouped = keep.tile([P, copies, G, O, PACK], BF16, align_bytes=64)
            for a in range(O_TILES):
                wt = turn_psum.tile([P, PACK, P], F32, tag="turned")
                w_words = w_sb[:, a, :].bitcast(F32)
                for t in range(PACK):
                    nc.tensor.transpose(wt[:, t, :], w_words[:, t : I : PACK], ident[:])
                nc.vector.tensor_scalar(
                    out=w_grouped[:, 0, :, a * P : (a + 1) * P, :],
                    in0=wt[:]
                    .rearrange("q t o -> q (t o)")
                    .bitcast(BF16)
                    .rearrange("q (t o g) -> q g o t", t=PACK, g=G),
                    scalar1=WEIGHT_COPIES[0],
                    scalar2=None,
                    op0=ALU.mult,
                )
            flat = w_grouped[:].rearrange("q s g o t -> q s (g o t)")
            nc.vector.tensor_scalar(
                out=flat[:, 1, :], in0=flat[:, 0, :],
                scalar1=WEIGHT_COPIES[1] / WEIGHT_COPIES[0], scalar2=None, op0=ALU.mult,
            )
            for s in range(copies):
                nc.vector.quantize_mx(
                    out=w_codes[:, s, :].bitcast(FP8X4), scales=w_scales[:, s, :], in_=flat[:, s, :]
                )

        turned, grouped, dist, bowl, gap_sq = {}, {}, {}, {}, {}
        x_codes, x_scales, basis_codes, basis_scales = {}, {}, {}, {}
        cube, inner, outer, basis, sums, result = {}, {}, {}, {}, {}, {}

        def turn_x(c):
            xt = turn_psum.tile([P, CHUNK_TILES[c], 2, P], F32, tag="turned")
            for j in range(CHUNK_TILES[c]):
                words = x_sb[:, FIRST_TILE[c] + j, :].bitcast(F32)
                for u in range(2):
                    nc.tensor.transpose(xt[:, j, u, :], words[:, u : I // 2 : 2], ident[:])
            turned[c] = xt

        def regroup_x(c):
            xg = late.tile([P, CHUNK_TILES[c] * TILE_W], BF16, align_bytes=64, tag="xg")
            nc.scalar.copy(
                out=xg[:].bitcast(F32).rearrange("p (j b u) -> p j b u", j=CHUNK_TILES[c], u=2),
                in_=turned[c][:].rearrange("p j u b -> p j b u"),
            )
            grouped[c] = xg

        def distances(c):
            d = work.tile([P, G, CHUNK_TILES[c] * TILE_W], F32, tag="dist")
            for g in range(G):
                nc.scalar.activation(
                    out=d[:, g, :], in_=grouped[c][:], func=FUNC.Abs,
                    bias=neg_grid[:, g : g + 1], scale=1.0,
                )
            dist[c] = d


        def gap_square(c):
            s = work.tile([P, G * CHUNK_TILES[c] * TILE_W], F32, tag="gap_sq")
            nc.scalar.activation(
                out=s[:], in_=dist[c][:].rearrange("p g w -> p (g w)"), func=FUNC.Square,
                bias=cube_bias[:], scale=ROOT_6,
            )
            gap_sq[c] = s

        def bowl_square(c):
            q = work.tile([P, G * CHUNK_TILES[c] * TILE_W], F32, tag="bowl")
            nc.scalar.activation(
                out=q[:], in_=dist[c][:].rearrange("p g w -> p (g w)"), func=FUNC.Square,
                bias=bowl_bias[:], scale=ROOT_12,
            )
            bowl[c] = q

        def cube_of_gap(c):
            m3 = work.tile([P, G * CHUNK_TILES[c] * TILE_W], F32, tag="cube")
            nc.vector.scalar_tensor_tensor(
                out=m3[:], in0=dist[c][:].rearrange("p g w -> p (g w)"), scalar=1.0,
                in1=gap_sq[c][:], op0=ALU.subtract, op1=ALU.mult,
            )
            cube[c] = m3

        def inner_piece(c):
            piece = work.tile([P, G * CHUNK_TILES[c] * TILE_W], BF16, tag="inner")
            nc.vector.scalar_tensor_tensor(
                out=piece[:], in0=bowl[c][:], scalar=0.25, in1=cube[c][:],
                op0=ALU.add, op1=ALU.add,
            )
            inner[c] = piece

        def outer_piece(c):
            piece = work.tile([P, G * CHUNK_TILES[c] * TILE_W], BF16, tag="outer")
            if c >= CHUNKS - SCALAR_OUTER_CHUNKS:
                nc.scalar.activation(out=piece[:], in_=cube[c][:], func=FUNC.Relu, scale=-1.0 / 3.0)
            else:
                nc.vector.tensor_scalar(
                    out=piece[:], in0=cube[c][:], scalar1=-1.0 / 3.0, scalar2=0.0,
                    op0=ALU.mult, op1=ALU.max,
                )
            outer[c] = piece

        def minimum(c):
            n = work.tile([P, G * CHUNK_TILES[c] * TILE_W], BF16, align_bytes=64, tag="basis")
            nc.vector.tensor_tensor(out=n[:], in0=inner[c][:], in1=outer[c][:], op=ALU.min)
            basis[c] = n

        def quantise_x(c):
            codes = late.tile([P, CHUNK_TILES[c] * P], U32, align_bytes=64, tag="x_codes", bufs=4)
            scales = late.tile([P, CHUNK_TILES[c] * P], U8, align_bytes=64, tag="x_scales", bufs=4)
            nc.vector.quantize_mx(
                out=codes[:].bitcast(FP8X4), scales=scales[:], in_=grouped[c][:]
            )
            x_codes[c], x_scales[c] = codes, scales

        def quantise_basis(c):
            codes = late.tile([P, G * CHUNK_TILES[c] * P], U32, align_bytes=64, tag="basis_codes")
            scales = late.tile([P, G * CHUNK_TILES[c] * P], U8, align_bytes=64, tag="basis_scales")
            nc.vector.quantize_mx(out=codes[:].bitcast(FP8X4), scales=scales[:], in_=basis[c][:])
            basis_codes[c], basis_scales[c] = codes, scales

        def multiply(c):
            tiles = CHUNK_TILES[c]
            for j in range(tiles):
                acc = sum_psum.tile([P, O], F32, tag="acc")
                rows = slice(j * P, (j + 1) * P)
                nc.tensor.matmul_mx(
                    out=acc[:],
                    lhsT=x_codes[c][:, rows].bitcast(FP8X4),
                    lhsT_scale=x_scales[c][:, rows],
                    rhs=w4_words[:].bitcast(FP4X4),
                    rhs_scale=w4_scales[:],
                    start=True,
                    stop=False,
                )
                for g in range(G):
                    rows = slice((g * tiles + j) * P, (g * tiles + j + 1) * P)
                    cols = slice(g * O, (g + 1) * O)
                    for s in range(copies):
                        nc.tensor.matmul_mx(
                            out=acc[:],
                            lhsT=basis_codes[c][:, rows].bitcast(FP8X4),
                            lhsT_scale=basis_scales[c][:, rows],
                            rhs=w_codes[:, s, cols].bitcast(FP8X4),
                            rhs_scale=w_scales[:, s, cols],
                            start=False,
                            stop=(g == G - 1 and s == copies - 1),
                        )
                sums[c, j] = acc

        def leave_psum(c, j):
            n = FIRST_TILE[c] + j
            if n % VECTOR_SHARE == VECTOR_SHARE - 1 and n < SCALAR_ONLY_FROM:
                nc.vector.tensor_scalar(
                    out=result[c][:, j, :], in0=sums[c, j][:], scalar1=BASE_FACTOR, scalar2=None,
                    op0=ALU.mult,
                )
            else:
                nc.scalar.activation(
                    out=result[c][:, j, :], in_=sums[c, j][:], func=FUNC.Copy, scale=BASE_FACTOR
                )

        def leave_first(c):
            scaled = late.tile([P, CHUNK_TILES[c], O], F32, tag="result")
            result[c] = scaled
            leave_psum(c, 0)

        def leave_second(c):
            if CHUNK_TILES[c] > 1:
                leave_psum(c, 1)

        def store(c):
            rows = slice(FIRST_TILE[c], FIRST_TILE[c] + CHUNK_TILES[c])
            nc.sync.dma_start(out=out_rows[:, rows, :], in_=result[c][:])

        def run(stage, c):
            if 0 <= c < CHUNKS:
                stage(c)

        def step(c):
            run(turn_x, c + 2)
            run(multiply, c - 2)
            run(distances, c + 1)
            run(cube_of_gap, c)
            run(regroup_x, c + 2)
            run(minimum, c - 1)
            run(gap_square, c + 1)
            run(inner_piece, c)
            run(leave_first, c - 3)
            run(quantise_x, c + 1)
            run(bowl_square, c + 1)
            run(outer_piece, c)
            run(leave_second, c - 3)
            run(store, c - 3)
            run(quantise_basis, c - 1)

        step(-2)
        prepare_spline_weight()
        for c in range(-1, CHUNKS + 3):
            step(c)
